import numpy as np
import ml_dtypes


def mxq(x, axis, fmt="e4m3"):
    dtype, down = {"e4m3": (ml_dtypes.float8_e4m3fn, 7), "e5m2": (ml_dtypes.float8_e5m2, 14)}[fmt]
    v = np.moveaxis(np.asarray(x, np.float32).astype(ml_dtypes.bfloat16).astype(np.float64), axis, -1)
    blocks = v.reshape(v.shape[:-1] + (-1, 32))
    amax = np.abs(blocks).max(-1, keepdims=True)
    byte = np.maximum(np.where(amax > 0, np.frexp(amax)[1] - 1 + 127, 0) - down, 1)
    scale = np.exp2(byte - 127.0)
    codes = (blocks / scale).astype(np.float32).astype(dtype).astype(np.float64)
    return np.moveaxis((codes * scale).reshape(v.shape), -1, axis)


WIDE = False


def mx_kscale(k):
    if not WIDE:
        return np.ones(k)
    levels = np.array([10, -10, 5, -5, 0])
    a = np.random.permutation(np.resize(levels, k // 512 * 4)).reshape(k // 512, 4)
    idx = np.arange(k)
    return np.exp2(a[idx // 512, idx % 128 // 32])


BF16 = ml_dtypes.bfloat16


def bf(x):
    return np.asarray(x, np.float32).astype(BF16)


def f64(x):
    return np.asarray(x).astype(np.float64)


E2M1 = np.array([0.0, 0.5, 1.0, 1.5, 2.0, 3.0, 4.0, 6.0, -0.0, -0.5, -1.0, -1.5, -2.0, -3.0, -4.0, -6.0])


def pack_weight(w, fmt):
    k, n = w.shape
    w = f64(bf(w)).reshape(k // 32, 32, n)
    amax = np.abs(w).max(1)
    if fmt == "e4m3":
        byte = np.frexp(amax)[1] - 1 + 127 - 7
    else:
        mant, ex = np.frexp(amax / 6.0)
        byte = np.where(mant > 0.5, ex, ex - 1) + 127
    byte = np.clip(np.where(amax > 0, byte, 1), 1, 254)
    scaled = (w * np.exp2(127.0 - byte)[:, None, :]).reshape(k, n).astype(np.float32)
    by_word = np.ascontiguousarray(scaled.reshape(k // 512, 128, 4, n).transpose(0, 1, 3, 2))
    if fmt == "e4m3":
        words = by_word.astype(ml_dtypes.float8_e4m3fn).view(np.uint8)
    else:
        c = by_word.astype(ml_dtypes.float4_e2m1fn).view(np.uint8) & 0xF
        words = c[..., 0::2] | (c[..., 1::2] << 4)
    return np.ascontiguousarray(words), np.ascontiguousarray(byte.astype(np.uint8).reshape(k // 512, 16, n))


def unpack_weight(words, scales, fmt):
    g, p, n, _ = words.shape
    if fmt == "e4m3":
        vals = np.ascontiguousarray(words).view(ml_dtypes.float8_e4m3fn).astype(np.float64)
    else:
        nib = np.empty((g, p, n, 4), np.uint8)
        nib[..., 0::2] = words & 0xF
        nib[..., 1::2] = words >> 4
        vals = E2M1[nib]
    vals = vals * np.repeat(np.exp2(scales.astype(np.float64) - 127.0), 8, axis=1)[..., None]
    return vals.transpose(0, 1, 3, 2).reshape(g * 512, n)


B, C0, C1, C2, C3, R0, R1, R2, R3, HID, NC = 128, 64, 64, 128, 256, 16, 8, 4, 2, 2048, 1024
D = 3 * (C0 + C1 + C2 + C3)
P_MEAN = 3.0
EPS_POOL = 1e-6
EPS_RMS = 1e-6
FMT = "e4m3"


def erf(z):
    a = np.minimum(np.abs(z), 6.0)
    term = a.copy()
    total = a.copy()
    for n in range(1, 150):
        term = term * (2.0 * a * a / (2 * n + 1))
        total = total + term
    return np.sign(z) * np.minimum(2.0 / np.sqrt(np.pi) * np.exp(-a * a) * total, 1.0)


def _pool(x):
    mean = np.mean(x, axis=(2, 3))
    max_val = np.max(x, axis=(2, 3))
    p = np.clip(np.abs(x), EPS_POOL, None) ** P_MEAN
    p_mean = np.mean(p, axis=(2, 3)) ** (1.0 / P_MEAN)
    return np.concatenate([mean, max_val, p_mean], axis=1)


def _butterfly(x, theta):
    h = x.shape[1] // 2
    a, b = x[:, :h], x[:, h:]
    c, s = np.cos(theta), np.sin(theta)
    return np.concatenate([c * a - s * b, s * a + c * b], axis=1)


def _feat(c, r):
    return bf(np.random.standard_normal((B, c, r, r)) + np.random.standard_normal((B, c, 1, 1)))


def setup_inputs():
    s = mx_kscale(D)
    f0 = _feat(C0, R0)
    f1 = _feat(C1, R1)
    f2 = _feat(C2, R2)
    f3 = _feat(C3, R3)
    theta = bf(np.random.standard_normal(D // 2) * 0.5)
    rms_w = bf((1.0 + 0.1 * np.random.standard_normal(D)) * s)
    w1_words, w1_scales = pack_weight(np.random.standard_normal((D, HID)) / np.sqrt(D) / s[:, None], FMT)
    b1 = bf(np.random.standard_normal(HID) * 0.3)
    w2_words, w2_scales = pack_weight(np.random.standard_normal((HID, NC)) * 1.5 / np.sqrt(HID), FMT)
    b2 = bf(np.random.standard_normal(NC) * 0.2)
    return {'f0': f0, 'f1': f1, 'f2': f2, 'f3': f3,
            'theta': theta,
            'rms_w': rms_w,
            'w1_words': w1_words, 'w1_scales': w1_scales,
            'b1': b1,
            'w2_words': w2_words, 'w2_scales': w2_scales,
            'b2': b2}


def reference(f0, f1, f2, f3, theta, rms_w, w1_words, w1_scales, b1, w2_words, w2_scales, b2):
    pooled = np.concatenate([_pool(f64(f0)), _pool(f64(f1)), _pool(f64(f2)), _pool(f64(f3))], axis=1)
    mixed = _butterfly(pooled, f64(theta))
    norm = mixed * (1.0 / np.sqrt(np.mean(mixed * mixed, axis=-1, keepdims=True) + EPS_RMS)) * f64(rms_w)
    a1 = (mxq(norm, 1, 'e4m3') @ unpack_weight(w1_words, w1_scales, FMT)) + f64(b1)
    h1 = 0.5 * a1 * (1.0 + erf(a1 / np.sqrt(2.0)))
    return (mxq(h1, 1, 'e4m3') @ unpack_weight(w2_words, w2_scales, FMT)) + f64(b2)

@@ -1,0 +1,389 @@
+import math
+from contextlib import ExitStack
+
+import concourse.mybir as mybir
+from concourse.masks import make_identity
+
+F32 = mybir.dt.float32
+BF16 = mybir.dt.bfloat16
+I32 = mybir.dt.int32
+U32 = mybir.dt.uint32
+U8 = mybir.dt.uint8
+FP8X4 = mybir.dt.float8_e4m3fn_x4
+ALU = mybir.AluOpType
+ACT = mybir.ActivationFunctionType
+AX = mybir.AxisListType
+
+P = 128
+PACK = 4
+K_PASS = P * PACK
+N_BANK = 512
+
+D = 1536
+HALF = D // 2
+HID = 2048
+NC = 1024
+FLOPS = 2 * P * (D * HID + HID * NC)
+
+EPS_POOL = 1e-6
+EPS_RMS = 1e-6
+EPS_BELOW = (134.0 / 128.0) * 2.0 ** -20
+SQUARE_FLOOR = EPS_POOL ** 3 / EPS_BELOW
+SIGN_OFF = 0x7FFF7FFF
+
+PIECE = 2048
+SCALAR_SUM_WINDOW = 64
+VECTOR_SUM_WINDOW = 256
+MAX_TAIL = 8
+MAX_LAG = 3
+SQ_BUFS = 3
+
+
+def tile_readouthead_kernel(
+    tc, f0, f1, f2, f3, theta, rms_w, w1_words, w1_scales, b1, w2_words, w2_scales, b2, out
+):
+    nc = tc.nc
+    k1_passes = D // K_PASS
+    k2_passes = HID // K_PASS
+    n1_banks = HID // N_BANK
+    n2_banks = NC // N_BANK
+
+    with ExitStack() as ctx:
+        ctx.enter_context(tc.manual_schedule())
+        keep = ctx.enter_context(tc.tile_pool(name="keep", bufs=1))
+        psum = ctx.enter_context(tc.psum_pool(name="psum", bufs=1))
+
+        w1_codes = keep.tile([P, k1_passes, HID], U32, align_bytes=64)
+        w1_planes = keep.tile([P, k1_passes, HID], U8, align_bytes=64)
+        w2_codes = keep.tile([P, k2_passes, NC], U32, align_bytes=64)
+        w2_planes = keep.tile([P, k2_passes, NC], U8, align_bytes=64)
+        nc.vector.memset(w1_planes[:].bitcast(I32), 0)
+        nc.vector.memset(w2_planes[:].bitcast(I32), 0)
+
+        identity = keep.tile([P, P], BF16)
+        make_identity(nc, identity[:])
+        minus_half = keep.tile([P, 1], F32)
+        nc.gpsimd.memset(minus_half[:], -0.5)
+
+        def load_pieces(label, fmap, base):
+            channels = fmap.shape[1]
+            window = fmap.shape[2] * fmap.shape[3]
+            rows = fmap.rearrange("b c h w -> b c (h w)")
+            step = min(channels, PIECE // window)
+            pieces = []
+            for c0 in range(0, channels, step):
+                x = keep.tile([P, step, window], BF16, name="%s_%d" % (label, c0))
+                nc.sync.dma_start(out=x[:], in_=rows[:, c0 : c0 + step, :])
+                pieces.append(
+                    dict(
+                        x=x,
+                        channels=step,
+                        window=window,
+                        mean_col=base + c0,
+                        max_col=base + channels + c0,
+                        cube_col=base // 3 + c0,
+                    )
+                )
+            return pieces
+
+        base0 = 0
+        base1 = base0 + 3 * f0.shape[1]
+        base2 = base1 + 3 * f1.shape[1]
+        base3 = base2 + 3 * f2.shape[1]
+        small_pieces = load_pieces("f3", f3, base3)
+        theta_all = keep.tile([P, HALF], BF16)
+        nc.sync.dma_start(out=theta_all[:], in_=theta.partition_broadcast(P))
+        small_pieces = small_pieces + load_pieces("f2", f2, base2) + load_pieces("f1", f1, base1)
+        f0_pieces = load_pieces("f0", f0, base0)
+        small_maps = [(f3, base3, 3), (f2, base2, 2), (f1, base1, 1)]
+        gain_all = keep.tile([P, D], BF16)
+        nc.sync.dma_start(out=gain_all[:], in_=rms_w.partition_broadcast(P))
+
+        def load_weight(codes, planes, words, scales):
+            by_row = scales.rearrange("g (quad r) n -> r quad g n", r=PACK)
+            for r in range(PACK):
+                nc.sync.dma_start(out=planes[r : P : 32, :, :].bitcast(I32), in_=by_row[r].bitcast(I32))
+            for g in range(words.shape[0]):
+                nc.sync.dma_start(
+                    out=codes[:, g, :].bitcast(I32),
+                    in_=words[g].rearrange("p n t -> p (n t)").bitcast(I32),
+                )
+
+        load_weight(w1_codes, w1_planes, w1_words, w1_scales)
+        b1_all = keep.tile([P, HID], BF16)
+        nc.sync.dma_start(out=b1_all[:], in_=b1.partition_broadcast(P))
+        load_weight(w2_codes, w2_planes, w2_words, w2_scales)
+        b2_all = keep.tile([P, NC], BF16)
+        nc.sync.dma_start(out=b2_all[:], in_=b2.partition_broadcast(P))
+
+        pooled = keep.tile([P, D], F32)
+        cube_sum = keep.tile([P, D // 3], F32)
+        cube_log = keep.tile([P, D // 3], F32)
+        plain_sum = keep.tile([P, D // 3], F32)
+        square_sum = keep.tile([P, 4], F32)
+        scrap = keep.tile([P, HALF], F32)
+        cos_all = keep.tile([P, HALF], F32)
+        sin_all = keep.tile([P, HALF], F32)
+        sin_b = keep.tile([P, HALF], F32)
+        cos_b = keep.tile([P, HALF], F32)
+        mixed = keep.tile([P, D], F32)
+
+        def squares(sq_pool, piece):
+            sq = sq_pool.tile([P, piece["channels"], piece["window"]], F32, tag="sq")
+            nc.scalar.activation(out=sq[:], in_=piece["x"][:], func=ACT.Square)
+            return sq
+
+        def means(piece):
+            x = piece["x"]
+            window = piece["window"]
+            col = piece["mean_col"]
+            if window >= SCALAR_SUM_WINDOW:
+                for c in range(piece["channels"]):
+                    nc.scalar.activation(
+                        out=scrap[:, 0:window],
+                        in_=x[:, c, :],
+                        func=ACT.Copy,
+                        scale=1.0 / window,
+                        accum_out=pooled[:, col + c : col + c + 1],
+                    )
+            else:
+                cube_col = piece["cube_col"]
+                nc.vector.tensor_reduce(
+                    out=plain_sum[:, cube_col : cube_col + piece["channels"]], in_=x[:], axis=AX.X, op=ALU.add
+                )
+
+        def sums_of_cubes(work, piece, sq):
+            channels = piece["channels"]
+            window = piece["window"]
+            col = piece["cube_col"]
+            flat = piece["x"][:].rearrange("p c s -> p (c s)")
+            size = work.tile([P, channels * window], BF16, tag="size")
+            nc.vector.tensor_scalar(
+                out=size[:].bitcast(I32), in0=flat.bitcast(I32), scalar1=SIGN_OFF, scalar2=None, op0=ALU.bitwise_and
+            )
+            clipped = work.tile([P, channels, window], BF16, tag="clipped")
+            nc.vector.tensor_scalar(
+                out=clipped[:].rearrange("p c s -> p (c s)"), in0=size[:], scalar1=EPS_BELOW, scalar2=None, op0=ALU.max
+            )
+            if window >= VECTOR_SUM_WINDOW:
+                for c in range(channels):
+                    nc.vector.scalar_tensor_tensor(
+                        out=sq[:, c, :],
+                        in0=sq[:, c, :],
+                        scalar=SQUARE_FLOOR,
+                        in1=clipped[:, c, :],
+                        op0=ALU.max,
+                        op1=ALU.mult,
+                        accum_out=cube_sum[:, col + c : col + c + 1],
+                    )
+            else:
+                sq_flat = sq[:].rearrange("p c s -> p (c s)")
+                nc.vector.scalar_tensor_tensor(
+                    out=sq_flat,
+                    in0=sq_flat,
+                    scalar=SQUARE_FLOOR,
+                    in1=clipped[:].rearrange("p c s -> p (c s)"),
+                    op0=ALU.max,
+                    op1=ALU.mult,
+                )
+                nc.vector.tensor_reduce(out=cube_sum[:, col : col + channels], in_=sq[:], axis=AX.X, op=ALU.add)
+
+        def maxima(work, piece):
+            channels = piece["channels"]
+            window = piece["window"]
+            col = piece["max_col"]
+            front = piece["x"]
+            level = 0
+            while window > MAX_TAIL:
+                window = window // 2
+                halved = work.tile([P, channels, window], BF16, tag="halved%d" % level)
+                nc.vector.tensor_tensor(
+                    out=halved[:], in0=front[:, :, 0:window], in1=front[:, :, window : 2 * window], op=ALU.max
+                )
+                front = halved
+                level += 1
+            nc.vector.tensor_reduce(out=pooled[:, col : col + channels], in_=front[:], axis=AX.X, op=ALU.max)
+
+        def power_means(maps):
+            for fmap, base, number in maps:
+                channels = fmap.shape[1]
+                window = fmap.shape[2] * fmap.shape[3]
+                cols = slice(base // 3, base // 3 + channels)
+                if window < SCALAR_SUM_WINDOW:
+                    nc.scalar.activation(
+                        out=pooled[:, base : base + channels], in_=plain_sum[:, cols], func=ACT.Copy, scale=1.0 / window
+                    )
+                nc.scalar.activation(out=cube_log[:, cols], in_=cube_sum[:, cols], func=ACT.Ln, scale=1.0 / window)
+            for fmap, base, number in maps:
+                channels = fmap.shape[1]
+                nc.scalar.activation(
+                    out=pooled[:, base + 2 * channels : base + 3 * channels],
+                    in_=cube_log[:, base // 3 : base // 3 + channels],
+                    func=ACT.Exp,
+                    scale=1.0 / 3.0,
+                )
+
+        def sums_of_squares(maps):
+            for fmap, base, number in maps:
+                width = 3 * fmap.shape[1]
+                nc.scalar.activation(
+                    out=scrap[:, 0:width],
+                    in_=pooled[:, base : base + width],
+                    func=ACT.Square,
+                    accum_out=square_sum[:, number : number + 1],
+                )
+
+        def rotate(work, lo, hi):
+            cos_a = work.tile([P, hi - lo], F32, tag="cos_a")
+            nc.vector.tensor_tensor(out=cos_a[:], in0=pooled[:, lo:hi], in1=cos_all[:, lo:hi], op=ALU.mult)
+            nc.vector.tensor_tensor(out=mixed[:, lo:hi], in0=cos_a[:], in1=sin_b[:, lo:hi], op=ALU.subtract)
+            sin_a = work.tile([P, hi - lo], F32, tag="sin_a")
+            nc.vector.tensor_tensor(out=sin_a[:], in0=pooled[:, lo:hi], in1=sin_all[:, lo:hi], op=ALU.mult)
+            nc.vector.tensor_tensor(
+                out=mixed[:, HALF + lo : HALF + hi], in0=sin_a[:], in1=cos_b[:, lo:hi], op=ALU.add
+            )
+
+        with tc.tile_pool(name="work", bufs=2) as work, tc.tile_pool(name="sq_pool", bufs=SQ_BUFS) as sq_pool:
+            with tc.tile_pool(name="trig", bufs=1) as trig:
+                for number, piece in enumerate(small_pieces):
+                    sq = squares(sq_pool, piece)
+                    means(piece)
+                    sums_of_cubes(work, piece, sq)
+                    maxima(work, piece)
+                    if number == 0:
+                        turns = trig.tile([P, HALF], I32)
+                        nc.vector.tensor_scalar(
+                            out=turns[:], in0=theta_all[:], scalar1=0.5 / math.pi, scalar2=None, op0=ALU.mult
+                        )
+                        angle = trig.tile([P, HALF], F32)
+                        nc.vector.scalar_tensor_tensor(
+                            out=angle[:],
+                            in0=turns[:],
+                            scalar=-2.0 * math.pi,
+                            in1=theta_all[:],
+                            op0=ALU.mult,
+                            op1=ALU.add,
+                        )
+                    if number == 1:
+                        sin_half = trig.tile([P, HALF], F32)
+                        nc.scalar.activation(out=sin_half[:], in_=angle[:], func=ACT.Sin, scale=0.5)
+                        two_cos_half = trig.tile([P, HALF], F32)
+                        nc.scalar.activation(out=two_cos_half[:], in_=angle[:], func=ACT.Sin, scale=0.25)
+                        nc.scalar.activation(out=two_cos_half[:], in_=two_cos_half[:], func=ACT.Square)
+                        nc.scalar.activation(
+                            out=two_cos_half[:], in_=two_cos_half[:], func=ACT.Copy, scale=-4.0, bias=2.0
+                        )
+                        nc.scalar.activation(out=cos_all[:], in_=sin_half[:], func=ACT.Square)
+                        nc.scalar.activation(out=cos_all[:], in_=cos_all[:], func=ACT.Copy, scale=-2.0, bias=1.0)
+                    if number == 2:
+                        nc.vector.tensor_tensor(out=sin_all[:], in0=sin_half[:], in1=two_cos_half[:], op=ALU.mult)
+
+            for number, piece in enumerate(f0_pieces):
+                sq = squares(sq_pool, piece)
+                means(piece)
+                sums_of_cubes(work, piece, sq)
+                if number >= MAX_LAG:
+                    maxima(work, f0_pieces[number - MAX_LAG])
+                if number == SQ_BUFS:
+                    power_means(small_maps)
+                    sums_of_squares(small_maps)
+                if number == SQ_BUFS + 1:
+                    nc.vector.tensor_tensor(out=sin_b[:], in0=pooled[:, HALF:D], in1=sin_all[:], op=ALU.mult)
+                    nc.vector.tensor_tensor(out=cos_b[:], in0=pooled[:, HALF:D], in1=cos_all[:], op=ALU.mult)
+                    rotate(work, base1, HALF)
+
+            for piece in f0_pieces[len(f0_pieces) - MAX_LAG :]:
+                maxima(work, piece)
+            power_means([(f0, base0, 0)])
+            nc.scalar.activation(out=scrap[:, 0:1], in_=minus_half[:], func=ACT.Gelu)
+            sums_of_squares([(f0, base0, 0)])
+            rotate(work, base0, base1)
+
+        tail = ctx.enter_context(tc.tile_pool(name="tail", bufs=1))
+        total = tail.tile([P, 1], F32)
+        nc.vector.tensor_reduce(out=total[:], in_=square_sum[:], axis=AX.X, op=ALU.add)
+        variance = tail.tile([P, 1], F32)
+        nc.vector.tensor_scalar(
+            out=variance[:], in0=total[:], scalar1=1.0 / D, scalar2=EPS_RMS, op0=ALU.mult, op1=ALU.add
+        )
+        inv_rms = tail.tile([P, 1], F32)
+        nc.gpsimd.tensor_tensor(out=inv_rms[:], in0=variance[:], in1=minus_half[:], op=ALU.pow)
+
+        def regroup(rows, g, copy):
+            turned = psum.tile([P, PACK, P], BF16, tag="turned%d" % g)
+            for t in range(PACK):
+                nc.tensor.transpose(
+                    out=turned[:, t, :], in_=rows[:, K_PASS * g + t : K_PASS * (g + 1) : PACK], identity=identity[:]
+                )
+            grouped = tail.tile([P, P, PACK], BF16, tag="grouped", bufs=k2_passes, align_bytes=64)
+            copy(out=grouped[:], in_=turned[:].rearrange("p t b -> p b t"))
+            return grouped
+
+        def quantise(grouped, g, codes, planes):
+            nc.vector.quantize_mx(
+                out=codes[:, g, :].bitcast(FP8X4),
+                scales=planes[:, g, :],
+                in_=grouped[:].rearrange("p b t -> p (b t)"),
+            )
+
+        norm = tail.tile([P, D], BF16)
+        for g in range(k1_passes):
+            cols = slice(K_PASS * g, K_PASS * (g + 1))
+            nc.vector.scalar_tensor_tensor(
+                out=norm[:, cols],
+                in0=mixed[:, cols],
+                scalar=inv_rms[:, 0:1],
+                in1=gain_all[:, cols],
+                op0=ALU.mult,
+                op1=ALU.mult,
+            )
+        norm_codes = tail.tile([P, k1_passes, P], U32, align_bytes=64)
+        norm_planes = tail.tile([P, k1_passes, P], U8, align_bytes=64)
+        norm_grouped = [regroup(norm, g, nc.scalar.copy) for g in range(k1_passes)]
+        for g in range(k1_passes):
+            quantise(norm_grouped[g], g, norm_codes, norm_planes)
+
+        a1_banks = [psum.tile([P, N_BANK], F32, name="a1_%d" % n, tag="acc%d" % n) for n in range(n1_banks)]
+        for g in range(k1_passes):
+            for n in range(n1_banks):
+                cols = slice(N_BANK * n, N_BANK * (n + 1))
+                nc.tensor.matmul_mx(
+                    out=a1_banks[n][:],
+                    lhsT=norm_codes[:, g, :].bitcast(FP8X4),
+                    lhsT_scale=norm_planes[:, g, :],
+                    rhs=w1_codes[:, g, cols].bitcast(FP8X4),
+                    rhs_scale=w1_planes[:, g, cols],
+                    start=(g == 0),
+                    stop=(g == k1_passes - 1),
+                )
+        h1 = tail.tile([P, HID], BF16)
+        for n in range(n1_banks):
+            cols = slice(N_BANK * n, N_BANK * (n + 1))
+            a1 = tail.tile([P, N_BANK], F32, tag="a1", bufs=2)
+            nc.vector.tensor_tensor(out=a1[:], in0=a1_banks[n][:], in1=b1_all[:, cols], op=ALU.add)
+            nc.scalar.activation(out=h1[:, cols], in_=a1[:], func=ACT.Gelu)
+
+        h1_codes = tail.tile([P, k2_passes, P], U32, align_bytes=64)
+        h1_planes = tail.tile([P, k2_passes, P], U8, align_bytes=64)
+        h1_grouped = [
+            regroup(h1, g, nc.vector.tensor_copy if g % 2 == 0 else nc.scalar.copy) for g in range(k2_passes)
+        ]
+        out_banks = [psum.tile([P, N_BANK], F32, name="out_%d" % n, tag="acc%d" % n) for n in range(n2_banks)]
+        for g in range(k2_passes):
+            quantise(h1_grouped[g], g, h1_codes, h1_planes)
+            for n in range(n2_banks):
+                cols = slice(N_BANK * n, N_BANK * (n + 1))
+                nc.tensor.matmul_mx(
+                    out=out_banks[n][:],
+                    lhsT=h1_codes[:, g, :].bitcast(FP8X4),
+                    lhsT_scale=h1_planes[:, g, :],
+                    rhs=w2_codes[:, g, cols].bitcast(FP8X4),
+                    rhs_scale=w2_planes[:, g, cols],
+                    start=(g == 0),
+                    stop=(g == k2_passes - 1),
+                )
+        for n in range(n2_banks):
+            cols = slice(N_BANK * n, N_BANK * (n + 1))
+            result = tail.tile([P, N_BANK], F32, tag="result", bufs=2)
+            nc.vector.tensor_tensor(out=result[:], in0=out_banks[n][:], in1=b2_all[:, cols], op=ALU.add)
+            nc.sync.dma_start(out=out[:, cols], in_=result[:])

@@ -32,8 +32,6 @@ SQUARE_FLOOR = EPS_POOL ** 3 / EPS_BELOW
 SIGN_OFF = 0x7FFF7FFF
 
 PIECE = 2048
-SCALAR_SUM_WINDOW = 64
-VECTOR_SUM_WINDOW = 256
 MAX_TAIL = 8
 MAX_LAG = 3
 SQ_BUFS = 3
@@ -62,14 +60,23 @@ def tile_readouthead_kernel(
 
         identity = keep.tile([P, P], BF16)
         make_identity(nc, identity[:])
+        identity_f32 = keep.tile([P, P], F32)
+        make_identity(nc, identity_f32[:])
         minus_half = keep.tile([P, 1], F32)
         nc.gpsimd.memset(minus_half[:], -0.5)
 
-        def load_pieces(label, fmap, base):
+        def load_pieces(label, fmap, base, mean_bank):
             channels = fmap.shape[1]
             window = fmap.shape[2] * fmap.shape[3]
             rows = fmap.rearrange("b c h w -> b c (h w)")
             step = min(channels, PIECE // window)
+            touched = (2 * P) // window if window < 2 * P else 1
+            counts = keep.tile([P, touched], F32, name="counts_%s" % label)
+            nc.vector.tensor_reduce(
+                out=counts[:], in_=identity_f32[:].rearrange("p (i j) -> p i j", i=touched), axis=AX.X, op=ALU.add
+            )
+            selector = keep.tile([P, touched], BF16, name="selector_%s" % label)
+            nc.vector.tensor_copy(out=selector[:], in_=counts[:])
             pieces = []
             for c0 in range(0, channels, step):
                 x = keep.tile([P, step, window], BF16, name="%s_%d" % (label, c0))
@@ -79,9 +86,10 @@ def tile_readouthead_kernel(
                         x=x,
                         channels=step,
                         window=window,
-                        mean_col=base + c0,
                         max_col=base + channels + c0,
-                        cube_col=base // 3 + c0,
+                        sum_col=base // 3 + c0,
+                        selector=selector,
+                        mean_bank=mean_bank,
                     )
                 )
             return pieces
@@ -90,12 +98,15 @@ def tile_readouthead_kernel(
         base1 = base0 + 3 * f0.shape[1]
         base2 = base1 + 3 * f1.shape[1]
         base3 = base2 + 3 * f2.shape[1]
-        small_pieces = load_pieces("f3", f3, base3)
+        small_sums = psum.tile([P, N_BANK], F32, tag="acc0")
+        f0_sums = psum.tile([P, N_BANK], F32, tag="acc1")
+        small_pieces = load_pieces("f3", f3, base3, small_sums)
         theta_all = keep.tile([P, HALF], BF16)
         nc.sync.dma_start(out=theta_all[:], in_=theta.partition_broadcast(P))
-        small_pieces = small_pieces + load_pieces("f2", f2, base2) + load_pieces("f1", f1, base1)
-        f0_pieces = load_pieces("f0", f0, base0)
-        small_maps = [(f3, base3, 3), (f2, base2, 2), (f1, base1, 1)]
+        small_pieces = small_pieces + load_pieces("f2", f2, base2, small_sums) + load_pieces("f1", f1, base1, small_sums)
+        f0_pieces = load_pieces("f0", f0, base0, f0_sums)
+        all_pieces = small_pieces + f0_pieces
+        small_maps = [(f3, base3, 3, small_sums), (f2, base2, 2, small_sums), (f1, base1, 1, small_sums)]
         gain_all = keep.tile([P, D], BF16)
         nc.sync.dma_start(out=gain_all[:], in_=rms_w.partition_broadcast(P))
 
@@ -119,7 +130,6 @@ def tile_readouthead_kernel(
         pooled = keep.tile([P, D], F32)
         cube_sum = keep.tile([P, D // 3], F32)
         cube_log = keep.tile([P, D // 3], F32)
-        plain_sum = keep.tile([P, D // 3], F32)
         square_sum = keep.tile([P, 4], F32)
         scrap = keep.tile([P, HALF], F32)
         cos_all = keep.tile([P, HALF], F32)
@@ -128,93 +138,133 @@ def tile_readouthead_kernel(
         cos_b = keep.tile([P, HALF], F32)
         mixed = keep.tile([P, D], F32)
 
+        def in_turn(*chains):
+            for k in range(max(len(chain) for chain in chains)):
+                for chain in chains:
+                    if k < len(chain):
+                        chain[k]()
+
+        def turn(turn_pool, piece):
+            words = piece["x"][:].rearrange("p c s -> p (c s)").bitcast(F32)
+            piece["turned"] = []
+            for first in range(0, words.shape[1], N_BANK):
+                bank = psum.tile([P, N_BANK // P, P], F32, tag="turned", bufs=4)
+                for j in range(N_BANK // P):
+                    nc.tensor.transpose(
+                        out=bank[:, j, :], in_=words[:, first + P * j : first + P * (j + 1)], identity=identity_f32[:]
+                    )
+                turned = turn_pool.tile([P, N_BANK // P, P], F32, tag="turned")
+                nc.scalar.copy(out=turned[:], in_=bank[:])
+                piece["turned"].append(turned)
+
+        def add_up(piece):
+            selector = piece["selector"]
+            touched = selector.shape[1]
+            col = piece["sum_col"]
+            for turned in piece["turned"]:
+                halves = turned[:].bitcast(BF16).rearrange("p j (b e) -> p j b e", e=2)
+                for j in range(N_BANK // P):
+                    for e in range(2):
+                        nc.tensor.matmul(
+                            out=piece["mean_bank"][:, col : col + touched],
+                            lhsT=halves[:, j, :, e],
+                            rhs=selector[:],
+                            start=(e == 0),
+                            stop=(e == 1),
+                        )
+                    col += touched
+
         def squares(sq_pool, piece):
             sq = sq_pool.tile([P, piece["channels"], piece["window"]], F32, tag="sq")
             nc.scalar.activation(out=sq[:], in_=piece["x"][:], func=ACT.Square)
-            return sq
+            piece["sq"] = sq
 
-        def means(piece):
-            x = piece["x"]
-            window = piece["window"]
-            col = piece["mean_col"]
-            if window >= SCALAR_SUM_WINDOW:
-                for c in range(piece["channels"]):
-                    nc.scalar.activation(
-                        out=scrap[:, 0:window],
-                        in_=x[:, c, :],
-                        func=ACT.Copy,
-                        scale=1.0 / window,
-                        accum_out=pooled[:, col + c : col + c + 1],
-                    )
-            else:
-                cube_col = piece["cube_col"]
-                nc.vector.tensor_reduce(
-                    out=plain_sum[:, cube_col : cube_col + piece["channels"]], in_=x[:], axis=AX.X, op=ALU.add
+        def size_chain(work, piece):
+            def strip_signs():
+                size = work.tile([P, piece["channels"] * piece["window"]], BF16, tag="size")
+                nc.vector.tensor_scalar(
+                    out=size[:].bitcast(I32),
+                    in0=piece["x"][:].rearrange("p c s -> p (c s)").bitcast(I32),
+                    scalar1=SIGN_OFF,
+                    scalar2=None,
+                    op0=ALU.bitwise_and,
                 )
+                piece["size"] = size
 
-        def sums_of_cubes(work, piece, sq):
-            channels = piece["channels"]
-            window = piece["window"]
-            col = piece["cube_col"]
-            flat = piece["x"][:].rearrange("p c s -> p (c s)")
-            size = work.tile([P, channels * window], BF16, tag="size")
-            nc.vector.tensor_scalar(
-                out=size[:].bitcast(I32), in0=flat.bitcast(I32), scalar1=SIGN_OFF, scalar2=None, op0=ALU.bitwise_and
-            )
-            clipped = work.tile([P, channels, window], BF16, tag="clipped")
-            nc.vector.tensor_scalar(
-                out=clipped[:].rearrange("p c s -> p (c s)"), in0=size[:], scalar1=EPS_BELOW, scalar2=None, op0=ALU.max
-            )
-            if window >= VECTOR_SUM_WINDOW:
-                for c in range(channels):
-                    nc.vector.scalar_tensor_tensor(
-                        out=sq[:, c, :],
-                        in0=sq[:, c, :],
-                        scalar=SQUARE_FLOOR,
-                        in1=clipped[:, c, :],
-                        op0=ALU.max,
-                        op1=ALU.mult,
-                        accum_out=cube_sum[:, col + c : col + c + 1],
-                    )
-            else:
-                sq_flat = sq[:].rearrange("p c s -> p (c s)")
-                nc.vector.scalar_tensor_tensor(
-                    out=sq_flat,
-                    in0=sq_flat,
-                    scalar=SQUARE_FLOOR,
-                    in1=clipped[:].rearrange("p c s -> p (c s)"),
+            def clip():
+                clipped = work.tile([P, piece["channels"], piece["window"]], BF16, tag="clipped")
+                nc.vector.tensor_scalar(
+                    out=clipped[:].rearrange("p c s -> p (c s)"),
+                    in0=piece["size"][:],
+                    scalar1=EPS_BELOW,
+                    scalar2=None,
                     op0=ALU.max,
-                    op1=ALU.mult,
                 )
-                nc.vector.tensor_reduce(out=cube_sum[:, col : col + channels], in_=sq[:], axis=AX.X, op=ALU.add)
+                piece["clipped"] = clipped
 
-        def maxima(work, piece):
+            return [strip_signs, clip]
+
+        def cube(sq, clipped, accum_out):
+            nc.vector.scalar_tensor_tensor(
+                out=sq, in0=sq, scalar=SQUARE_FLOOR, in1=clipped, op0=ALU.max, op1=ALU.mult, accum_out=accum_out
+            )
+
+        def channel_cubes(piece):
+            col = piece["sum_col"]
+            return [
+                lambda c=c: cube(piece["sq"][:, c, :], piece["clipped"][:, c, :], cube_sum[:, col + c : col + c + 1])
+                for c in range(piece["channels"])
+            ]
+
+        def piece_cubes(piece):
+            col = piece["sum_col"]
+            return [
+                lambda: cube(
+                    piece["sq"][:].rearrange("p c s -> p (c s)"),
+                    piece["clipped"][:].rearrange("p c s -> p (c s)"),
+                    None,
+                ),
+                lambda: nc.vector.tensor_reduce(
+                    out=cube_sum[:, col : col + piece["channels"]], in_=piece["sq"][:], axis=AX.X, op=ALU.add
+                ),
+            ]
+
+        def max_chain(work, piece):
             channels = piece["channels"]
-            window = piece["window"]
             col = piece["max_col"]
-            front = piece["x"]
-            level = 0
-            while window > MAX_TAIL:
-                window = window // 2
-                halved = work.tile([P, channels, window], BF16, tag="halved%d" % level)
+            state = dict(front=piece["x"], window=piece["window"], level=0)
+
+            def halve():
+                window = state["window"] // 2
+                front = state["front"]
+                halved = work.tile([P, channels, window], BF16, tag="halved%d" % state["level"], bufs=MAX_LAG)
                 nc.vector.tensor_tensor(
                     out=halved[:], in0=front[:, :, 0:window], in1=front[:, :, window : 2 * window], op=ALU.max
                 )
-                front = halved
-                level += 1
-            nc.vector.tensor_reduce(out=pooled[:, col : col + channels], in_=front[:], axis=AX.X, op=ALU.max)
+                state["front"] = halved
+                state["window"] = window
+                state["level"] = state["level"] + 1
 
-        def power_means(maps):
-            for fmap, base, number in maps:
+            def finish():
+                nc.vector.tensor_reduce(
+                    out=pooled[:, col : col + channels], in_=state["front"][:], axis=AX.X, op=ALU.max
+                )
+
+            halvings = 0
+            while piece["window"] > MAX_TAIL * 2 ** halvings:
+                halvings += 1
+            return [halve] * halvings + [finish]
+
+        def means_and_power_means(maps):
+            for fmap, base, slot, sums in maps:
                 channels = fmap.shape[1]
                 window = fmap.shape[2] * fmap.shape[3]
                 cols = slice(base // 3, base // 3 + channels)
-                if window < SCALAR_SUM_WINDOW:
-                    nc.scalar.activation(
-                        out=pooled[:, base : base + channels], in_=plain_sum[:, cols], func=ACT.Copy, scale=1.0 / window
-                    )
+                nc.scalar.activation(
+                    out=pooled[:, base : base + channels], in_=sums[:, cols], func=ACT.Copy, scale=1.0 / window
+                )
                 nc.scalar.activation(out=cube_log[:, cols], in_=cube_sum[:, cols], func=ACT.Ln, scale=1.0 / window)
-            for fmap, base, number in maps:
+            for fmap, base, slot, sums in maps:
                 channels = fmap.shape[1]
                 nc.scalar.activation(
                     out=pooled[:, base + 2 * channels : base + 3 * channels],
@@ -224,32 +274,38 @@ def tile_readouthead_kernel(
                 )
 
         def sums_of_squares(maps):
-            for fmap, base, number in maps:
+            for fmap, base, slot, sums in maps:
                 width = 3 * fmap.shape[1]
                 nc.scalar.activation(
                     out=scrap[:, 0:width],
                     in_=pooled[:, base : base + width],
                     func=ACT.Square,
-                    accum_out=square_sum[:, number : number + 1],
+                    accum_out=square_sum[:, slot : slot + 1],
                 )
 
         def rotate(work, lo, hi):
             cos_a = work.tile([P, hi - lo], F32, tag="cos_a")
-            nc.vector.tensor_tensor(out=cos_a[:], in0=pooled[:, lo:hi], in1=cos_all[:, lo:hi], op=ALU.mult)
-            nc.vector.tensor_tensor(out=mixed[:, lo:hi], in0=cos_a[:], in1=sin_b[:, lo:hi], op=ALU.subtract)
             sin_a = work.tile([P, hi - lo], F32, tag="sin_a")
+            nc.vector.tensor_tensor(out=cos_a[:], in0=pooled[:, lo:hi], in1=cos_all[:, lo:hi], op=ALU.mult)
             nc.vector.tensor_tensor(out=sin_a[:], in0=pooled[:, lo:hi], in1=sin_all[:, lo:hi], op=ALU.mult)
+            nc.vector.tensor_tensor(out=mixed[:, lo:hi], in0=cos_a[:], in1=sin_b[:, lo:hi], op=ALU.subtract)
             nc.vector.tensor_tensor(
                 out=mixed[:, HALF + lo : HALF + hi], in0=sin_a[:], in1=cos_b[:, lo:hi], op=ALU.add
             )
 
-        with tc.tile_pool(name="work", bufs=2) as work, tc.tile_pool(name="sq_pool", bufs=SQ_BUFS) as sq_pool:
+        with tc.tile_pool(name="work", bufs=2) as work, tc.tile_pool(name="sq_pool", bufs=SQ_BUFS) as sq_pool, tc.tile_pool(
+            name="turn_pool", bufs=4
+        ) as turn_pool:
+            in_turn(size_chain(work, all_pieces[0]))
             with tc.tile_pool(name="trig", bufs=1) as trig:
                 for number, piece in enumerate(small_pieces):
-                    sq = squares(sq_pool, piece)
-                    means(piece)
-                    sums_of_cubes(work, piece, sq)
-                    maxima(work, piece)
+                    turn(turn_pool, piece)
+                    squares(sq_pool, piece)
+                    if number > 0:
+                        add_up(small_pieces[number - 1])
+                    cubes, sums = piece_cubes(piece)
+                    strip_signs, clip = size_chain(work, all_pieces[number + 1])
+                    in_turn([cubes, strip_signs, sums, clip], max_chain(work, piece))
                     if number == 0:
                         turns = trig.tile([P, HALF], I32)
                         nc.vector.tensor_scalar(
@@ -269,34 +325,38 @@ def tile_readouthead_kernel(
                         nc.scalar.activation(out=sin_half[:], in_=angle[:], func=ACT.Sin, scale=0.5)
                         two_cos_half = trig.tile([P, HALF], F32)
                         nc.scalar.activation(out=two_cos_half[:], in_=angle[:], func=ACT.Sin, scale=0.25)
+                        nc.scalar.activation(out=cos_all[:], in_=sin_half[:], func=ACT.Square)
                         nc.scalar.activation(out=two_cos_half[:], in_=two_cos_half[:], func=ACT.Square)
+                        nc.scalar.activation(out=cos_all[:], in_=cos_all[:], func=ACT.Copy, scale=-2.0, bias=1.0)
                         nc.scalar.activation(
                             out=two_cos_half[:], in_=two_cos_half[:], func=ACT.Copy, scale=-4.0, bias=2.0
                         )
-                        nc.scalar.activation(out=cos_all[:], in_=sin_half[:], func=ACT.Square)
-                        nc.scalar.activation(out=cos_all[:], in_=cos_all[:], func=ACT.Copy, scale=-2.0, bias=1.0)
                     if number == 2:
                         nc.vector.tensor_tensor(out=sin_all[:], in0=sin_half[:], in1=two_cos_half[:], op=ALU.mult)
 
             for number, piece in enumerate(f0_pieces):
-                sq = squares(sq_pool, piece)
-                means(piece)
-                sums_of_cubes(work, piece, sq)
+                turn(turn_pool, piece)
+                squares(sq_pool, piece)
+                add_up(all_pieces[len(small_pieces) + number - 1])
+                others = []
+                if number + 1 < len(f0_pieces):
+                    others = others + size_chain(work, f0_pieces[number + 1])
                 if number >= MAX_LAG:
-                    maxima(work, f0_pieces[number - MAX_LAG])
+                    others = others + max_chain(work, f0_pieces[number - MAX_LAG])
+                in_turn(channel_cubes(piece), others)
                 if number == SQ_BUFS:
-                    power_means(small_maps)
+                    means_and_power_means(small_maps)
                     sums_of_squares(small_maps)
                 if number == SQ_BUFS + 1:
                     nc.vector.tensor_tensor(out=sin_b[:], in0=pooled[:, HALF:D], in1=sin_all[:], op=ALU.mult)
                     nc.vector.tensor_tensor(out=cos_b[:], in0=pooled[:, HALF:D], in1=cos_all[:], op=ALU.mult)
                     rotate(work, base1, HALF)
+            add_up(f0_pieces[len(f0_pieces) - 1])
 
-            for piece in f0_pieces[len(f0_pieces) - MAX_LAG :]:
-                maxima(work, piece)
-            power_means([(f0, base0, 0)])
+            in_turn(*[max_chain(work, piece) for piece in f0_pieces[len(f0_pieces) - MAX_LAG :]])
+            means_and_power_means([(f0, base0, 0, f0_sums)])
             nc.scalar.activation(out=scrap[:, 0:1], in_=minus_half[:], func=ACT.Gelu)
-            sums_of_squares([(f0, base0, 0)])
+            sums_of_squares([(f0, base0, 0, f0_sums)])
             rotate(work, base0, base1)
 
         tail = ctx.enter_context(tc.tile_pool(name="tail", bufs=1))
@@ -310,7 +370,7 @@ def tile_readouthead_kernel(
         nc.gpsimd.tensor_tensor(out=inv_rms[:], in0=variance[:], in1=minus_half[:], op=ALU.pow)
 
         def regroup(rows, g, copy):
-            turned = psum.tile([P, PACK, P], BF16, tag="turned%d" % g)
+            turned = psum.tile([P, PACK, P], BF16, tag="turned", bufs=4)
             for t in range(PACK):
                 nc.tensor.transpose(
                     out=turned[:, t, :], in_=rows[:, K_PASS * g + t : K_PASS * (g + 1) : PACK], identity=identity[:]

@@ -34,6 +34,9 @@ SIGN_OFF = 0x7FFF7FFF
 PIECE = 2048
 MAX_TAIL = 8
 MAX_LAG = 3
+SCALAR_SUM_WINDOW = 64
+SUM_LAG = 2
+ROOTS_AT = 5
 SQ_BUFS = 3
 
 
@@ -62,6 +65,8 @@ def tile_readouthead_kernel(
         make_identity(nc, identity[:])
         identity_f32 = keep.tile([P, P], F32)
         make_identity(nc, identity_f32[:])
+        theta_rows = keep.tile([P, P], BF16)
+        nc.gpsimd.memset(theta_rows[:], 0.0)
         minus_half = keep.tile([P, 1], F32)
         nc.gpsimd.memset(minus_half[:], -0.5)
 
@@ -100,12 +105,13 @@ def tile_readouthead_kernel(
         base3 = base2 + 3 * f2.shape[1]
         small_sums = psum.tile([P, N_BANK], F32, tag="acc0")
         f0_sums = psum.tile([P, N_BANK], F32, tag="acc1")
-        small_pieces = load_pieces("f3", f3, base3, small_sums)
-        theta_all = keep.tile([P, HALF], BF16)
-        nc.sync.dma_start(out=theta_all[:], in_=theta.partition_broadcast(P))
-        small_pieces = small_pieces + load_pieces("f2", f2, base2, small_sums) + load_pieces("f1", f1, base1, small_sums)
-        f0_pieces = load_pieces("f0", f0, base0, f0_sums)
-        all_pieces = small_pieces + f0_pieces
+        small_pieces = (
+            load_pieces("f1", f1, base1, small_sums)
+            + load_pieces("f2", f2, base2, small_sums)
+            + load_pieces("f3", f3, base3, small_sums)
+        )
+        nc.sync.dma_start(out=theta_rows[0 : HALF // P, :], in_=theta.rearrange("(j p) -> j p", p=P))
+        all_pieces = small_pieces + load_pieces("f0", f0, base0, f0_sums)
         small_maps = [(f3, base3, 3, small_sums), (f2, base2, 2, small_sums), (f1, base1, 1, small_sums)]
         gain_all = keep.tile([P, D], BF16)
         nc.sync.dma_start(out=gain_all[:], in_=rms_w.partition_broadcast(P))
@@ -132,8 +138,9 @@ def tile_readouthead_kernel(
         cube_log = keep.tile([P, D // 3], F32)
         square_sum = keep.tile([P, 4], F32)
         scrap = keep.tile([P, HALF], F32)
-        cos_all = keep.tile([P, HALF], F32)
-        sin_all = keep.tile([P, HALF], F32)
+        cos_sin = keep.tile([P, 2 * HALF], F32)
+        cos_all = cos_sin[:, 0:HALF]
+        sin_all = cos_sin[:, HALF : 2 * HALF]
         sin_b = keep.tile([P, HALF], F32)
         cos_b = keep.tile([P, HALF], F32)
         mixed = keep.tile([P, D], F32)
@@ -216,6 +223,16 @@ def tile_readouthead_kernel(
                 for c in range(piece["channels"])
             ]
 
+        def channel_sums(piece):
+            col = piece["sum_col"]
+            for c in range(piece["channels"]):
+                nc.scalar.activation(
+                    out=piece["sq"][:, c, :],
+                    in_=piece["sq"][:, c, :],
+                    func=ACT.Copy,
+                    accum_out=cube_sum[:, col + c : col + c + 1],
+                )
+
         def piece_cubes(piece):
             col = piece["sum_col"]
             return [
@@ -293,78 +310,112 @@ def tile_readouthead_kernel(
                 out=mixed[:, HALF + lo : HALF + hi], in0=sin_a[:], in1=cos_b[:, lo:hi], op=ALU.add
             )
 
+        def trig_stage(trig, stage, made):
+            chunks = HALF // P
+            if stage == 0:
+                theta_bank = psum.tile([P, P], BF16, tag="turned", bufs=4)
+                nc.tensor.transpose(out=theta_bank[:], in_=theta_rows[:], identity=identity[:])
+                theta_cols = trig.tile([P, chunks], F32)
+                nc.vector.tensor_copy(out=theta_cols[:], in_=theta_bank[:, 0:chunks])
+                turns = trig.tile([P, chunks], I32)
+                nc.vector.tensor_scalar(
+                    out=turns[:], in0=theta_cols[:], scalar1=0.5 / math.pi, scalar2=None, op0=ALU.mult
+                )
+                angle = trig.tile([P, chunks], F32)
+                nc.vector.scalar_tensor_tensor(
+                    out=angle[:], in0=turns[:], scalar=-2.0 * math.pi, in1=theta_cols[:], op0=ALU.mult, op1=ALU.add
+                )
+                made["angle"] = angle
+            if stage == 1:
+                angle = made["angle"]
+                cos_cols = trig.tile([P, chunks], F32)
+                sin_half = trig.tile([P, chunks], F32)
+                two_cos_half = trig.tile([P, chunks], F32)
+                nc.scalar.activation(out=sin_half[:], in_=angle[:], func=ACT.Sin, scale=0.5)
+                nc.scalar.activation(out=two_cos_half[:], in_=angle[:], func=ACT.Sin, scale=0.25)
+                nc.scalar.activation(out=cos_cols[:], in_=sin_half[:], func=ACT.Square)
+                nc.scalar.activation(out=two_cos_half[:], in_=two_cos_half[:], func=ACT.Square)
+                nc.scalar.activation(out=cos_cols[:], in_=cos_cols[:], func=ACT.Copy, scale=-2.0, bias=1.0)
+                nc.scalar.activation(out=two_cos_half[:], in_=two_cos_half[:], func=ACT.Copy, scale=-4.0, bias=2.0)
+                made["cos_cols"] = cos_cols
+                made["sin_half"] = sin_half
+                made["two_cos_half"] = two_cos_half
+            if stage == 2:
+                sin_cols = trig.tile([P, chunks], F32)
+                nc.vector.tensor_tensor(
+                    out=sin_cols[:], in0=made["sin_half"][:], in1=made["two_cos_half"][:], op=ALU.mult
+                )
+                made["sin_cols"] = sin_cols
+            if stage == 3:
+                columns = [made["cos_cols"][:, j : j + 1] for j in range(chunks)]
+                columns = columns + [made["sin_cols"][:, j : j + 1] for j in range(chunks)]
+                for first in range(0, 2 * chunks, N_BANK // P):
+                    spread = psum.tile([P, N_BANK // P, P], F32, tag="turned", bufs=4)
+                    for j in range(N_BANK // P):
+                        nc.tensor.matmul(
+                            out=spread[:, j, :],
+                            lhsT=columns[first + j].to_broadcast([P, P]),
+                            rhs=identity_f32[:],
+                            start=True,
+                            stop=True,
+                        )
+                    nc.scalar.copy(
+                        out=cos_sin[:, P * first : P * first + N_BANK], in_=spread[:].rearrange("p j n -> p (j n)")
+                    )
+
         with tc.tile_pool(name="work", bufs=2) as work, tc.tile_pool(name="sq_pool", bufs=SQ_BUFS) as sq_pool, tc.tile_pool(
             name="turn_pool", bufs=4
-        ) as turn_pool:
+        ) as turn_pool, tc.tile_pool(name="trig", bufs=1) as trig:
+            made = dict()
+            first_f0 = len(small_pieces)
             in_turn(size_chain(work, all_pieces[0]))
-            with tc.tile_pool(name="trig", bufs=1) as trig:
-                for number, piece in enumerate(small_pieces):
-                    turn(turn_pool, piece)
-                    squares(sq_pool, piece)
-                    if number > 0:
-                        add_up(small_pieces[number - 1])
-                    cubes, sums = piece_cubes(piece)
-                    strip_signs, clip = size_chain(work, all_pieces[number + 1])
-                    in_turn([cubes, strip_signs, sums, clip], max_chain(work, piece))
-                    if number == 0:
-                        turns = trig.tile([P, HALF], I32)
-                        nc.vector.tensor_scalar(
-                            out=turns[:], in0=theta_all[:], scalar1=0.5 / math.pi, scalar2=None, op0=ALU.mult
-                        )
-                        angle = trig.tile([P, HALF], F32)
-                        nc.vector.scalar_tensor_tensor(
-                            out=angle[:],
-                            in0=turns[:],
-                            scalar=-2.0 * math.pi,
-                            in1=theta_all[:],
-                            op0=ALU.mult,
-                            op1=ALU.add,
-                        )
-                    if number == 1:
-                        sin_half = trig.tile([P, HALF], F32)
-                        nc.scalar.activation(out=sin_half[:], in_=angle[:], func=ACT.Sin, scale=0.5)
-                        two_cos_half = trig.tile([P, HALF], F32)
-                        nc.scalar.activation(out=two_cos_half[:], in_=angle[:], func=ACT.Sin, scale=0.25)
-                        nc.scalar.activation(out=cos_all[:], in_=sin_half[:], func=ACT.Square)
-                        nc.scalar.activation(out=two_cos_half[:], in_=two_cos_half[:], func=ACT.Square)
-                        nc.scalar.activation(out=cos_all[:], in_=cos_all[:], func=ACT.Copy, scale=-2.0, bias=1.0)
-                        nc.scalar.activation(
-                            out=two_cos_half[:], in_=two_cos_half[:], func=ACT.Copy, scale=-4.0, bias=2.0
-                        )
-                    if number == 2:
-                        nc.vector.tensor_tensor(out=sin_all[:], in0=sin_half[:], in1=two_cos_half[:], op=ALU.mult)
-
-            for number, piece in enumerate(f0_pieces):
+            squares(sq_pool, all_pieces[0])
+            for number, piece in enumerate(all_pieces):
+                if number >= SUM_LAG and all_pieces[number - SUM_LAG]["window"] == SCALAR_SUM_WINDOW:
+                    channel_sums(all_pieces[number - SUM_LAG])
+                if number + 1 < len(all_pieces):
+                    squares(sq_pool, all_pieces[number + 1])
                 turn(turn_pool, piece)
-                squares(sq_pool, piece)
-                add_up(all_pieces[len(small_pieces) + number - 1])
-                others = []
-                if number + 1 < len(f0_pieces):
-                    others = others + size_chain(work, f0_pieces[number + 1])
-                if number >= MAX_LAG:
-                    others = others + max_chain(work, f0_pieces[number - MAX_LAG])
-                in_turn(channel_cubes(piece), others)
-                if number == SQ_BUFS:
+                if number > 0:
+                    add_up(all_pieces[number - 1])
+                ahead = size_chain(work, all_pieces[number + 1]) if number + 1 < len(all_pieces) else []
+                if number >= first_f0:
+                    behind = max_chain(work, all_pieces[number - MAX_LAG]) if number >= first_f0 + MAX_LAG else []
+                    in_turn(channel_cubes(piece), ahead + behind)
+                else:
+                    cubes, sums = piece_cubes(piece)
+                    if piece["window"] == SCALAR_SUM_WINDOW:
+                        in_turn(max_chain(work, piece), [cubes] + ahead)
+                    else:
+                        in_turn(max_chain(work, piece), [cubes, ahead[0], sums, ahead[1]])
+                if first_f0 <= number < first_f0 + 4:
+                    trig_stage(trig, number - first_f0, made)
+                if number == first_f0 + ROOTS_AT:
                     means_and_power_means(small_maps)
                     sums_of_squares(small_maps)
-                if number == SQ_BUFS + 1:
-                    nc.vector.tensor_tensor(out=sin_b[:], in0=pooled[:, HALF:D], in1=sin_all[:], op=ALU.mult)
-                    nc.vector.tensor_tensor(out=cos_b[:], in0=pooled[:, HALF:D], in1=cos_all[:], op=ALU.mult)
+                if number == first_f0 + ROOTS_AT + 1:
+                    nc.vector.tensor_tensor(out=sin_b[:], in0=pooled[:, HALF:D], in1=sin_all, op=ALU.mult)
+                    nc.vector.tensor_tensor(out=cos_b[:], in0=pooled[:, HALF:D], in1=cos_all, op=ALU.mult)
                     rotate(work, base1, HALF)
-            add_up(f0_pieces[len(f0_pieces) - 1])
+            add_up(all_pieces[len(all_pieces) - 1])
 
-            in_turn(*[max_chain(work, piece) for piece in f0_pieces[len(f0_pieces) - MAX_LAG :]])
+            in_turn(*[max_chain(work, piece) for piece in all_pieces[len(all_pieces) - MAX_LAG :]])
             means_and_power_means([(f0, base0, 0, f0_sums)])
             nc.scalar.activation(out=scrap[:, 0:1], in_=minus_half[:], func=ACT.Gelu)
             sums_of_squares([(f0, base0, 0, f0_sums)])
             rotate(work, base0, base1)
 
         tail = ctx.enter_context(tc.tile_pool(name="tail", bufs=1))
-        total = tail.tile([P, 1], F32)
-        nc.vector.tensor_reduce(out=total[:], in_=square_sum[:], axis=AX.X, op=ALU.add)
+        shares = tail.tile([P, 4], F32)
         variance = tail.tile([P, 1], F32)
         nc.vector.tensor_scalar(
-            out=variance[:], in0=total[:], scalar1=1.0 / D, scalar2=EPS_RMS, op0=ALU.mult, op1=ALU.add
+            out=shares[:],
+            in0=square_sum[:],
+            scalar1=1.0 / D,
+            scalar2=EPS_RMS,
+            op0=ALU.mult,
+            op1=ALU.add,
+            accum_out=variance[:],
         )
         inv_rms = tail.tile([P, 1], F32)
         nc.gpsimd.tensor_tensor(out=inv_rms[:], in0=variance[:], in1=minus_half[:], op=ALU.pow)

@@ -69,6 +69,8 @@ def tile_readouthead_kernel(
         nc.gpsimd.memset(theta_rows[:], 0.0)
         minus_half = keep.tile([P, 1], F32)
         nc.gpsimd.memset(minus_half[:], -0.5)
+        first_sine = keep.tile([P, 1], F32)
+        nc.scalar.activation(out=first_sine[:], in_=minus_half[:], func=ACT.Sin)
 
         def load_pieces(label, fmap, base, mean_bank):
             channels = fmap.shape[1]
@@ -106,9 +108,9 @@ def tile_readouthead_kernel(
         small_sums = psum.tile([P, N_BANK], F32, tag="acc0")
         f0_sums = psum.tile([P, N_BANK], F32, tag="acc1")
         small_pieces = (
-            load_pieces("f1", f1, base1, small_sums)
+            load_pieces("f3", f3, base3, small_sums)
+            + load_pieces("f1", f1, base1, small_sums)
             + load_pieces("f2", f2, base2, small_sums)
-            + load_pieces("f3", f3, base3, small_sums)
         )
         nc.sync.dma_start(out=theta_rows[0 : HALF // P, :], in_=theta.rearrange("(j p) -> j p", p=P))
         all_pieces = small_pieces + load_pieces("f0", f0, base0, f0_sums)
@@ -300,15 +302,32 @@ def tile_readouthead_kernel(
                     accum_out=square_sum[:, slot : slot + 1],
                 )
 
-        def rotate(work, lo, hi):
+        def rotate(work, lo, hi, between):
             cos_a = work.tile([P, hi - lo], F32, tag="cos_a")
             sin_a = work.tile([P, hi - lo], F32, tag="sin_a")
             nc.vector.tensor_tensor(out=cos_a[:], in0=pooled[:, lo:hi], in1=cos_all[:, lo:hi], op=ALU.mult)
             nc.vector.tensor_tensor(out=sin_a[:], in0=pooled[:, lo:hi], in1=sin_all[:, lo:hi], op=ALU.mult)
+            between()
             nc.vector.tensor_tensor(out=mixed[:, lo:hi], in0=cos_a[:], in1=sin_b[:, lo:hi], op=ALU.subtract)
             nc.vector.tensor_tensor(
                 out=mixed[:, HALF + lo : HALF + hi], in0=sin_a[:], in1=cos_b[:, lo:hi], op=ALU.add
             )
+
+        inv_rms = keep.tile([P, 1], F32)
+
+        def inverse_rms():
+            shares = keep.tile([P, 4], F32)
+            variance = keep.tile([P, 1], F32)
+            nc.vector.tensor_scalar(
+                out=shares[:],
+                in0=square_sum[:],
+                scalar1=1.0 / D,
+                scalar2=EPS_RMS,
+                op0=ALU.mult,
+                op1=ALU.add,
+                accum_out=variance[:],
+            )
+            nc.gpsimd.tensor_tensor(out=inv_rms[:], in0=variance[:], in1=minus_half[:], op=ALU.pow)
 
         def trig_stage(trig, stage, made):
             chunks = HALF // P
@@ -396,36 +415,24 @@ def tile_readouthead_kernel(
                 if number == first_f0 + ROOTS_AT + 1:
                     nc.vector.tensor_tensor(out=sin_b[:], in0=pooled[:, HALF:D], in1=sin_all, op=ALU.mult)
                     nc.vector.tensor_tensor(out=cos_b[:], in0=pooled[:, HALF:D], in1=cos_all, op=ALU.mult)
-                    rotate(work, base1, HALF)
+                    rotate(work, base1, HALF, lambda: None)
             add_up(all_pieces[len(all_pieces) - 1])
 
             in_turn(*[max_chain(work, piece) for piece in all_pieces[len(all_pieces) - MAX_LAG :]])
             means_and_power_means([(f0, base0, 0, f0_sums)])
             nc.scalar.activation(out=scrap[:, 0:1], in_=minus_half[:], func=ACT.Gelu)
             sums_of_squares([(f0, base0, 0, f0_sums)])
-            rotate(work, base0, base1)
+            rotate(work, base0, base1, inverse_rms)
 
         tail = ctx.enter_context(tc.tile_pool(name="tail", bufs=1))
-        shares = tail.tile([P, 4], F32)
-        variance = tail.tile([P, 1], F32)
-        nc.vector.tensor_scalar(
-            out=shares[:],
-            in0=square_sum[:],
-            scalar1=1.0 / D,
-            scalar2=EPS_RMS,
-            op0=ALU.mult,
-            op1=ALU.add,
-            accum_out=variance[:],
-        )
-        inv_rms = tail.tile([P, 1], F32)
-        nc.gpsimd.tensor_tensor(out=inv_rms[:], in0=variance[:], in1=minus_half[:], op=ALU.pow)
+
+        def sorted_by_t(cols):
+            return cols.rearrange("b (p t) -> b t p", t=PACK)
 
         def regroup(rows, g, copy):
             turned = psum.tile([P, PACK, P], BF16, tag="turned", bufs=4)
             for t in range(PACK):
-                nc.tensor.transpose(
-                    out=turned[:, t, :], in_=rows[:, K_PASS * g + t : K_PASS * (g + 1) : PACK], identity=identity[:]
-                )
+                nc.tensor.transpose(out=turned[:, t, :], in_=rows[:, g, t, :], identity=identity[:])
             grouped = tail.tile([P, P, PACK], BF16, tag="grouped", bufs=k2_passes, align_bytes=64)
             copy(out=grouped[:], in_=turned[:].rearrange("p t b -> p b t"))
             return grouped
@@ -437,14 +444,14 @@ def tile_readouthead_kernel(
                 in_=grouped[:].rearrange("p b t -> p (b t)"),
             )
 
-        norm = tail.tile([P, D], BF16)
+        norm = tail.tile([P, k1_passes, PACK, P], BF16)
         for g in range(k1_passes):
             cols = slice(K_PASS * g, K_PASS * (g + 1))
             nc.vector.scalar_tensor_tensor(
-                out=norm[:, cols],
-                in0=mixed[:, cols],
+                out=norm[:, g, :, :],
+                in0=sorted_by_t(mixed[:, cols]),
                 scalar=inv_rms[:, 0:1],
-                in1=gain_all[:, cols],
+                in1=sorted_by_t(gain_all[:, cols]),
                 op0=ALU.mult,
                 op1=ALU.mult,
             )
@@ -467,12 +474,15 @@ def tile_readouthead_kernel(
                     start=(g == 0),
                     stop=(g == k1_passes - 1),
                 )
-        h1 = tail.tile([P, HID], BF16)
+        assert N_BANK == K_PASS
+        h1 = tail.tile([P, k2_passes, PACK, P], BF16)
         for n in range(n1_banks):
             cols = slice(N_BANK * n, N_BANK * (n + 1))
-            a1 = tail.tile([P, N_BANK], F32, tag="a1", bufs=2)
-            nc.vector.tensor_tensor(out=a1[:], in0=a1_banks[n][:], in1=b1_all[:, cols], op=ALU.add)
-            nc.scalar.activation(out=h1[:, cols], in_=a1[:], func=ACT.Gelu)
+            a1 = tail.tile([P, PACK, P], F32, tag="a1", bufs=2)
+            nc.vector.tensor_tensor(
+                out=a1[:], in0=sorted_by_t(a1_banks[n][:]), in1=sorted_by_t(b1_all[:, cols]), op=ALU.add
+            )
+            nc.scalar.activation(out=h1[:, n, :, :], in_=a1[:], func=ACT.Gelu)
 
         h1_codes = tail.tile([P, k2_passes, P], U32, align_bytes=64)
         h1_planes = tail.tile([P, k2_passes, P], U8, align_bytes=64)

@@ -33,11 +33,11 @@ SIGN_OFF = 0x7FFF7FFF
 
 PIECE = 2048
 MAX_TAIL = 8
-MAX_LAG = 3
+MAX_LAG = 4
 SCALAR_SUM_WINDOW = 64
 SUM_LAG = 2
 ROOTS_AT = 5
-SQ_BUFS = 3
+SQ_BUFS = 4
 
 
 def tile_readouthead_kernel(
@@ -426,13 +426,12 @@ def tile_readouthead_kernel(
 
         tail = ctx.enter_context(tc.tile_pool(name="tail", bufs=1))
 
-        def sorted_by_t(cols):
-            return cols.rearrange("b (p t) -> b t p", t=PACK)
-
         def regroup(rows, g, copy):
             turned = psum.tile([P, PACK, P], BF16, tag="turned", bufs=4)
             for t in range(PACK):
-                nc.tensor.transpose(out=turned[:, t, :], in_=rows[:, g, t, :], identity=identity[:])
+                nc.tensor.transpose(
+                    out=turned[:, t, :], in_=rows[:, K_PASS * g + t : K_PASS * (g + 1) : PACK], identity=identity[:]
+                )
             grouped = tail.tile([P, P, PACK], BF16, tag="grouped", bufs=k2_passes, align_bytes=64)
             copy(out=grouped[:], in_=turned[:].rearrange("p t b -> p b t"))
             return grouped
@@ -444,14 +443,14 @@ def tile_readouthead_kernel(
                 in_=grouped[:].rearrange("p b t -> p (b t)"),
             )
 
-        norm = tail.tile([P, k1_passes, PACK, P], BF16)
+        norm = tail.tile([P, D], BF16)
         for g in range(k1_passes):
             cols = slice(K_PASS * g, K_PASS * (g + 1))
             nc.vector.scalar_tensor_tensor(
-                out=norm[:, g, :, :],
-                in0=sorted_by_t(mixed[:, cols]),
+                out=norm[:, cols],
+                in0=mixed[:, cols],
                 scalar=inv_rms[:, 0:1],
-                in1=sorted_by_t(gain_all[:, cols]),
+                in1=gain_all[:, cols],
                 op0=ALU.mult,
                 op1=ALU.mult,
             )
@@ -474,15 +473,12 @@ def tile_readouthead_kernel(
                     start=(g == 0),
                     stop=(g == k1_passes - 1),
                 )
-        assert N_BANK == K_PASS
-        h1 = tail.tile([P, k2_passes, PACK, P], BF16)
+        h1 = tail.tile([P, HID], BF16)
         for n in range(n1_banks):
             cols = slice(N_BANK * n, N_BANK * (n + 1))
-            a1 = tail.tile([P, PACK, P], F32, tag="a1", bufs=2)
-            nc.vector.tensor_tensor(
-                out=a1[:], in0=sorted_by_t(a1_banks[n][:]), in1=sorted_by_t(b1_all[:, cols]), op=ALU.add
-            )
-            nc.scalar.activation(out=h1[:, n, :, :], in_=a1[:], func=ACT.Gelu)
+            a1 = tail.tile([P, N_BANK], F32, tag="a1", bufs=2)
+            nc.vector.tensor_tensor(out=a1[:], in0=a1_banks[n][:], in1=b1_all[:, cols], op=ALU.add)
+            nc.scalar.activation(out=h1[:, cols], in_=a1[:], func=ACT.Gelu)
 
         h1_codes = tail.tile([P, k2_passes, P], U32, align_bytes=64)
         h1_planes = tail.tile([P, k2_passes, P], U8, align_bytes=64)

import math
from contextlib import ExitStack

import concourse.mybir as mybir
from concourse.masks import make_identity

F32 = mybir.dt.float32
BF16 = mybir.dt.bfloat16
I32 = mybir.dt.int32
U32 = mybir.dt.uint32
U8 = mybir.dt.uint8
FP8X4 = mybir.dt.float8_e4m3fn_x4
ALU = mybir.AluOpType
ACT = mybir.ActivationFunctionType
AX = mybir.AxisListType

P = 128
PACK = 4
K_PASS = P * PACK
N_BANK = 512

D = 1536
HALF = D // 2
HID = 2048
NC = 1024
FLOPS = 2 * P * (D * HID + HID * NC)

EPS_POOL = 1e-6
EPS_RMS = 1e-6
EPS_BELOW = (134.0 / 128.0) * 2.0 ** -20
SQUARE_FLOOR = EPS_POOL ** 3 / EPS_BELOW
SIGN_OFF = 0x7FFF7FFF

PIECE = 2048
MAX_TAIL = 8
MAX_LAG = 4
SCALAR_SUM_WINDOW = 64
SUM_LAG = 2
ROOTS_AT = 5
SQ_BUFS = 4


def tile_readouthead_kernel(
    tc, f0, f1, f2, f3, theta, rms_w, w1_words, w1_scales, b1, w2_words, w2_scales, b2, out
):
    nc = tc.nc
    k1_passes = D // K_PASS
    k2_passes = HID // K_PASS
    n1_banks = HID // N_BANK
    n2_banks = NC // N_BANK

    with ExitStack() as ctx:
        ctx.enter_context(tc.manual_schedule())
        keep = ctx.enter_context(tc.tile_pool(name="keep", bufs=1))
        psum = ctx.enter_context(tc.psum_pool(name="psum", bufs=1))

        w1_codes = keep.tile([P, k1_passes, HID], U32, align_bytes=64)
        w1_planes = keep.tile([P, k1_passes, HID], U8, align_bytes=64)
        w2_codes = keep.tile([P, k2_passes, NC], U32, align_bytes=64)
        w2_planes = keep.tile([P, k2_passes, NC], U8, align_bytes=64)
        nc.vector.memset(w1_planes[:].bitcast(I32), 0)
        nc.vector.memset(w2_planes[:].bitcast(I32), 0)

        identity = keep.tile([P, P], BF16)
        make_identity(nc, identity[:])
        identity_f32 = keep.tile([P, P], F32)
        make_identity(nc, identity_f32[:])
        theta_rows = keep.tile([P, P], BF16)
        nc.gpsimd.memset(theta_rows[:], 0.0)
        minus_half = keep.tile([P, 1], F32)
        nc.gpsimd.memset(minus_half[:], -0.5)
        first_sine = keep.tile([P, 1], F32)
        nc.scalar.activation(out=first_sine[:], in_=minus_half[:], func=ACT.Sin)

        def load_pieces(label, fmap, base, mean_bank):
            channels = fmap.shape[1]
            window = fmap.shape[2] * fmap.shape[3]
            rows = fmap.rearrange("b c h w -> b c (h w)")
            step = min(channels, PIECE // window)
            touched = (2 * P) // window if window < 2 * P else 1
            counts = keep.tile([P, touched], F32, name="counts_%s" % label)
            nc.vector.tensor_reduce(
                out=counts[:], in_=identity_f32[:].rearrange("p (i j) -> p i j", i=touched), axis=AX.X, op=ALU.add
            )
            selector = keep.tile([P, touched], BF16, name="selector_%s" % label)
            nc.vector.tensor_copy(out=selector[:], in_=counts[:])
            pieces = []
            for c0 in range(0, channels, step):
                x = keep.tile([P, step, window], BF16, name="%s_%d" % (label, c0))
                nc.sync.dma_start(out=x[:], in_=rows[:, c0 : c0 + step, :])
                pieces.append(
                    dict(
                        x=x,
                        channels=step,
                        window=window,
                        max_col=base + channels + c0,
                        sum_col=base // 3 + c0,
                        selector=selector,
                        mean_bank=mean_bank,
                    )
                )
            return pieces

        base0 = 0
        base1 = base0 + 3 * f0.shape[1]
        base2 = base1 + 3 * f1.shape[1]
        base3 = base2 + 3 * f2.shape[1]
        small_sums = psum.tile([P, N_BANK], F32, tag="acc0")
        f0_sums = psum.tile([P, N_BANK], F32, tag="acc1")
        small_pieces = (
            load_pieces("f3", f3, base3, small_sums)
            + load_pieces("f1", f1, base1, small_sums)
            + load_pieces("f2", f2, base2, small_sums)
        )
        nc.sync.dma_start(out=theta_rows[0 : HALF // P, :], in_=theta.rearrange("(j p) -> j p", p=P))
        all_pieces = small_pieces + load_pieces("f0", f0, base0, f0_sums)
        small_maps = [(f3, base3, 3, small_sums), (f2, base2, 2, small_sums), (f1, base1, 1, small_sums)]
        gain_all = keep.tile([P, D], BF16)
        nc.sync.dma_start(out=gain_all[:], in_=rms_w.partition_broadcast(P))

        def load_weight(codes, planes, words, scales):
            by_row = scales.rearrange("g (quad r) n -> r quad g n", r=PACK)
            for r in range(PACK):
                nc.sync.dma_start(out=planes[r : P : 32, :, :].bitcast(I32), in_=by_row[r].bitcast(I32))
            for g in range(words.shape[0]):
                nc.sync.dma_start(
                    out=codes[:, g, :].bitcast(I32),
                    in_=words[g].rearrange("p n t -> p (n t)").bitcast(I32),
                )

        load_weight(w1_codes, w1_planes, w1_words, w1_scales)
        b1_all = keep.tile([P, HID], BF16)
        nc.sync.dma_start(out=b1_all[:], in_=b1.partition_broadcast(P))
        load_weight(w2_codes, w2_planes, w2_words, w2_scales)
        b2_all = keep.tile([P, NC], BF16)
        nc.sync.dma_start(out=b2_all[:], in_=b2.partition_broadcast(P))

        pooled = keep.tile([P, D], F32)
        cube_sum = keep.tile([P, D // 3], F32)
        cube_log = keep.tile([P, D // 3], F32)
        square_sum = keep.tile([P, 4], F32)
        scrap = keep.tile([P, HALF], F32)
        cos_sin = keep.tile([P, 2 * HALF], F32)
        cos_all = cos_sin[:, 0:HALF]
        sin_all = cos_sin[:, HALF : 2 * HALF]
        sin_b = keep.tile([P, HALF], F32)
        cos_b = keep.tile([P, HALF], F32)
        mixed = keep.tile([P, D], F32)

        def in_turn(*chains):
            for k in range(max(len(chain) for chain in chains)):
                for chain in chains:
                    if k < len(chain):
                        chain[k]()

        def turn(turn_pool, piece):
            words = piece["x"][:].rearrange("p c s -> p (c s)").bitcast(F32)
            piece["turned"] = []
            for first in range(0, words.shape[1], N_BANK):
                bank = psum.tile([P, N_BANK // P, P], F32, tag="turned", bufs=4)
                for j in range(N_BANK // P):
                    nc.tensor.transpose(
                        out=bank[:, j, :], in_=words[:, first + P * j : first + P * (j + 1)], identity=identity_f32[:]
                    )
                turned = turn_pool.tile([P, N_BANK // P, P], F32, tag="turned")
                nc.scalar.copy(out=turned[:], in_=bank[:])
                piece["turned"].append(turned)

        def add_up(piece):
            selector = piece["selector"]
            touched = selector.shape[1]
            col = piece["sum_col"]
            for turned in piece["turned"]:
                halves = turned[:].bitcast(BF16).rearrange("p j (b e) -> p j b e", e=2)
                for j in range(N_BANK // P):
                    for e in range(2):
                        nc.tensor.matmul(
                            out=piece["mean_bank"][:, col : col + touched],
                            lhsT=halves[:, j, :, e],
                            rhs=selector[:],
                            start=(e == 0),
                            stop=(e == 1),
                        )
                    col += touched

        def squares(sq_pool, piece):
            sq = sq_pool.tile([P, piece["channels"], piece["window"]], F32, tag="sq")
            nc.scalar.activation(out=sq[:], in_=piece["x"][:], func=ACT.Square)
            piece["sq"] = sq

        def size_chain(work, piece):
            def strip_signs():
                size = work.tile([P, piece["channels"] * piece["window"]], BF16, tag="size")
                nc.vector.tensor_scalar(
                    out=size[:].bitcast(I32),
                    in0=piece["x"][:].rearrange("p c s -> p (c s)").bitcast(I32),
                    scalar1=SIGN_OFF,
                    scalar2=None,
                    op0=ALU.bitwise_and,
                )
                piece["size"] = size

            def clip():
                clipped = work.tile([P, piece["channels"], piece["window"]], BF16, tag="clipped")
                nc.vector.tensor_scalar(
                    out=clipped[:].rearrange("p c s -> p (c s)"),
                    in0=piece["size"][:],
                    scalar1=EPS_BELOW,
                    scalar2=None,
                    op0=ALU.max,
                )
                piece["clipped"] = clipped

            return [strip_signs, clip]

        def cube(sq, clipped, accum_out):
            nc.vector.scalar_tensor_tensor(
                out=sq, in0=sq, scalar=SQUARE_FLOOR, in1=clipped, op0=ALU.max, op1=ALU.mult, accum_out=accum_out
            )

        def channel_cubes(piece):
            col = piece["sum_col"]
            return [
                lambda c=c: cube(piece["sq"][:, c, :], piece["clipped"][:, c, :], cube_sum[:, col + c : col + c + 1])
                for c in range(piece["channels"])
            ]

        def channel_sums(piece):
            col = piece["sum_col"]
            for c in range(piece["channels"]):
                nc.scalar.activation(
                    out=piece["sq"][:, c, :],
                    in_=piece["sq"][:, c, :],
                    func=ACT.Copy,
                    accum_out=cube_sum[:, col + c : col + c + 1],
                )

        def piece_cubes(piece):
            col = piece["sum_col"]
            return [
                lambda: cube(
                    piece["sq"][:].rearrange("p c s -> p (c s)"),
                    piece["clipped"][:].rearrange("p c s -> p (c s)"),
                    None,
                ),
                lambda: nc.vector.tensor_reduce(
                    out=cube_sum[:, col : col + piece["channels"]], in_=piece["sq"][:], axis=AX.X, op=ALU.add
                ),
            ]

        def max_chain(work, piece):
            channels = piece["channels"]
            col = piece["max_col"]
            state = dict(front=piece["x"], window=piece["window"], level=0)

            def halve():
                window = state["window"] // 2
                front = state["front"]
                halved = work.tile([P, channels, window], BF16, tag="halved%d" % state["level"], bufs=MAX_LAG)
                nc.vector.tensor_tensor(
                    out=halved[:], in0=front[:, :, 0:window], in1=front[:, :, window : 2 * window], op=ALU.max
                )
                state["front"] = halved
                state["window"] = window
                state["level"] = state["level"] + 1

            def finish():
                nc.vector.tensor_reduce(
                    out=pooled[:, col : col + channels], in_=state["front"][:], axis=AX.X, op=ALU.max
                )

            halvings = 0
            while piece["window"] > MAX_TAIL * 2 ** halvings:
                halvings += 1
            return [halve] * halvings + [finish]

        def means_and_power_means(maps):
            for fmap, base, slot, sums in maps:
                channels = fmap.shape[1]
                window = fmap.shape[2] * fmap.shape[3]
                cols = slice(base // 3, base // 3 + channels)
                nc.scalar.activation(
                    out=pooled[:, base : base + channels], in_=sums[:, cols], func=ACT.Copy, scale=1.0 / window
                )
                nc.scalar.activation(out=cube_log[:, cols], in_=cube_sum[:, cols], func=ACT.Ln, scale=1.0 / window)
            for fmap, base, slot, sums in maps:
                channels = fmap.shape[1]
                nc.scalar.activation(
                    out=pooled[:, base + 2 * channels : base + 3 * channels],
                    in_=cube_log[:, base // 3 : base // 3 + channels],
                    func=ACT.Exp,
                    scale=1.0 / 3.0,
                )

        def sums_of_squares(maps):
            for fmap, base, slot, sums in maps:
                width = 3 * fmap.shape[1]
                nc.scalar.activation(
                    out=scrap[:, 0:width],
                    in_=pooled[:, base : base + width],
                    func=ACT.Square,
                    accum_out=square_sum[:, slot : slot + 1],
                )

        def rotate(work, lo, hi, between):
            cos_a = work.tile([P, hi - lo], F32, tag="cos_a")
            sin_a = work.tile([P, hi - lo], F32, tag="sin_a")
            nc.vector.tensor_tensor(out=cos_a[:], in0=pooled[:, lo:hi], in1=cos_all[:, lo:hi], op=ALU.mult)
            nc.vector.tensor_tensor(out=sin_a[:], in0=pooled[:, lo:hi], in1=sin_all[:, lo:hi], op=ALU.mult)
            between()
            nc.vector.tensor_tensor(out=mixed[:, lo:hi], in0=cos_a[:], in1=sin_b[:, lo:hi], op=ALU.subtract)
            nc.vector.tensor_tensor(
                out=mixed[:, HALF + lo : HALF + hi], in0=sin_a[:], in1=cos_b[:, lo:hi], op=ALU.add
            )

        inv_rms = keep.tile([P, 1], F32)

        def inverse_rms():
            shares = keep.tile([P, 4], F32)
            variance = keep.tile([P, 1], F32)
            nc.vector.tensor_scalar(
                out=shares[:],
                in0=square_sum[:],
                scalar1=1.0 / D,
                scalar2=EPS_RMS,
                op0=ALU.mult,
                op1=ALU.add,
                accum_out=variance[:],
            )
            nc.gpsimd.tensor_tensor(out=inv_rms[:], in0=variance[:], in1=minus_half[:], op=ALU.pow)

        def trig_stage(trig, stage, made):
            chunks = HALF // P
            if stage == 0:
                theta_bank = psum.tile([P, P], BF16, tag="turned", bufs=4)
                nc.tensor.transpose(out=theta_bank[:], in_=theta_rows[:], identity=identity[:])
                theta_cols = trig.tile([P, chunks], F32)
                nc.vector.tensor_copy(out=theta_cols[:], in_=theta_bank[:, 0:chunks])
                turns = trig.tile([P, chunks], I32)
                nc.vector.tensor_scalar(
                    out=turns[:], in0=theta_cols[:], scalar1=0.5 / math.pi, scalar2=None, op0=ALU.mult
                )
                angle = trig.tile([P, chunks], F32)
                nc.vector.scalar_tensor_tensor(
                    out=angle[:], in0=turns[:], scalar=-2.0 * math.pi, in1=theta_cols[:], op0=ALU.mult, op1=ALU.add
                )
                made["angle"] = angle
            if stage == 1:
                angle = made["angle"]
                cos_cols = trig.tile([P, chunks], F32)
                sin_half = trig.tile([P, chunks], F32)
                two_cos_half = trig.tile([P, chunks], F32)
                nc.scalar.activation(out=sin_half[:], in_=angle[:], func=ACT.Sin, scale=0.5)
                nc.scalar.activation(out=two_cos_half[:], in_=angle[:], func=ACT.Sin, scale=0.25)
                nc.scalar.activation(out=cos_cols[:], in_=sin_half[:], func=ACT.Square)
                nc.scalar.activation(out=two_cos_half[:], in_=two_cos_half[:], func=ACT.Square)
                nc.scalar.activation(out=cos_cols[:], in_=cos_cols[:], func=ACT.Copy, scale=-2.0, bias=1.0)
                nc.scalar.activation(out=two_cos_half[:], in_=two_cos_half[:], func=ACT.Copy, scale=-4.0, bias=2.0)
                made["cos_cols"] = cos_cols
                made["sin_half"] = sin_half
                made["two_cos_half"] = two_cos_half
            if stage == 2:
                sin_cols = trig.tile([P, chunks], F32)
                nc.vector.tensor_tensor(
                    out=sin_cols[:], in0=made["sin_half"][:], in1=made["two_cos_half"][:], op=ALU.mult
                )
                made["sin_cols"] = sin_cols
            if stage == 3:
                columns = [made["cos_cols"][:, j : j + 1] for j in range(chunks)]
                columns = columns + [made["sin_cols"][:, j : j + 1] for j in range(chunks)]
                for first in range(0, 2 * chunks, N_BANK // P):
                    spread = psum.tile([P, N_BANK // P, P], F32, tag="turned", bufs=4)
                    for j in range(N_BANK // P):
                        nc.tensor.matmul(
                            out=spread[:, j, :],
                            lhsT=columns[first + j].to_broadcast([P, P]),
                            rhs=identity_f32[:],
                            start=True,
                            stop=True,
                        )
                    nc.scalar.copy(
                        out=cos_sin[:, P * first : P * first + N_BANK], in_=spread[:].rearrange("p j n -> p (j n)")
                    )

        with tc.tile_pool(name="work", bufs=2) as work, tc.tile_pool(name="sq_pool", bufs=SQ_BUFS) as sq_pool, tc.tile_pool(
            name="turn_pool", bufs=4
        ) as turn_pool, tc.tile_pool(name="trig", bufs=1) as trig:
            made = dict()
            first_f0 = len(small_pieces)
            in_turn(size_chain(work, all_pieces[0]))
            squares(sq_pool, all_pieces[0])
            for number, piece in enumerate(all_pieces):
                if number >= SUM_LAG and all_pieces[number - SUM_LAG]["window"] == SCALAR_SUM_WINDOW:
                    channel_sums(all_pieces[number - SUM_LAG])
                if number + 1 < len(all_pieces):
                    squares(sq_pool, all_pieces[number + 1])
                turn(turn_pool, piece)
                if number > 0:
                    add_up(all_pieces[number - 1])
                ahead = size_chain(work, all_pieces[number + 1]) if number + 1 < len(all_pieces) else []
                if number >= first_f0:
                    behind = max_chain(work, all_pieces[number - MAX_LAG]) if number >= first_f0 + MAX_LAG else []
                    in_turn(channel_cubes(piece), ahead + behind)
                else:
                    cubes, sums = piece_cubes(piece)
                    if piece["window"] == SCALAR_SUM_WINDOW:
                        in_turn(max_chain(work, piece), [cubes] + ahead)
                    else:
                        in_turn(max_chain(work, piece), [cubes, ahead[0], sums, ahead[1]])
                if first_f0 <= number < first_f0 + 4:
                    trig_stage(trig, number - first_f0, made)
                if number == first_f0 + ROOTS_AT:
                    means_and_power_means(small_maps)
                    sums_of_squares(small_maps)
                if number == first_f0 + ROOTS_AT + 1:
                    nc.vector.tensor_tensor(out=sin_b[:], in0=pooled[:, HALF:D], in1=sin_all, op=ALU.mult)
                    nc.vector.tensor_tensor(out=cos_b[:], in0=pooled[:, HALF:D], in1=cos_all, op=ALU.mult)
                    rotate(work, base1, HALF, lambda: None)
            add_up(all_pieces[len(all_pieces) - 1])

            in_turn(*[max_chain(work, piece) for piece in all_pieces[len(all_pieces) - MAX_LAG :]])
            means_and_power_means([(f0, base0, 0, f0_sums)])
            nc.scalar.activation(out=scrap[:, 0:1], in_=minus_half[:], func=ACT.Gelu)
            sums_of_squares([(f0, base0, 0, f0_sums)])
            rotate(work, base0, base1, inverse_rms)

        tail = ctx.enter_context(tc.tile_pool(name="tail", bufs=1))

        def regroup(rows, g, copy):
            turned = psum.tile([P, PACK, P], BF16, tag="turned", bufs=4)
            for t in range(PACK):
                nc.tensor.transpose(
                    out=turned[:, t, :], in_=rows[:, K_PASS * g + t : K_PASS * (g + 1) : PACK], identity=identity[:]
                )
            grouped = tail.tile([P, P, PACK], BF16, tag="grouped", bufs=k2_passes, align_bytes=64)
            copy(out=grouped[:], in_=turned[:].rearrange("p t b -> p b t"))
            return grouped

        def quantise(grouped, g, codes, planes):
            nc.vector.quantize_mx(
                out=codes[:, g, :].bitcast(FP8X4),
                scales=planes[:, g, :],
                in_=grouped[:].rearrange("p b t -> p (b t)"),
            )

        norm = tail.tile([P, D], BF16)
        for g in range(k1_passes):
            cols = slice(K_PASS * g, K_PASS * (g + 1))
            nc.vector.scalar_tensor_tensor(
                out=norm[:, cols],
                in0=mixed[:, cols],
                scalar=inv_rms[:, 0:1],
                in1=gain_all[:, cols],
                op0=ALU.mult,
                op1=ALU.mult,
            )
        norm_codes = tail.tile([P, k1_passes, P], U32, align_bytes=64)
        norm_planes = tail.tile([P, k1_passes, P], U8, align_bytes=64)
        norm_grouped = [regroup(norm, g, nc.scalar.copy) for g in range(k1_passes)]
        for g in range(k1_passes):
            quantise(norm_grouped[g], g, norm_codes, norm_planes)

        a1_banks = [psum.tile([P, N_BANK], F32, name="a1_%d" % n, tag="acc%d" % n) for n in range(n1_banks)]
        for g in range(k1_passes):
            for n in range(n1_banks):
                cols = slice(N_BANK * n, N_BANK * (n + 1))
                nc.tensor.matmul_mx(
                    out=a1_banks[n][:],
                    lhsT=norm_codes[:, g, :].bitcast(FP8X4),
                    lhsT_scale=norm_planes[:, g, :],
                    rhs=w1_codes[:, g, cols].bitcast(FP8X4),
                    rhs_scale=w1_planes[:, g, cols],
                    start=(g == 0),
                    stop=(g == k1_passes - 1),
                )
        h1 = tail.tile([P, HID], BF16)
        for n in range(n1_banks):
            cols = slice(N_BANK * n, N_BANK * (n + 1))
            a1 = tail.tile([P, N_BANK], F32, tag="a1", bufs=2)
            nc.vector.tensor_tensor(out=a1[:], in0=a1_banks[n][:], in1=b1_all[:, cols], op=ALU.add)
            nc.scalar.activation(out=h1[:, cols], in_=a1[:], func=ACT.Gelu)

        h1_codes = tail.tile([P, k2_passes, P], U32, align_bytes=64)
        h1_planes = tail.tile([P, k2_passes, P], U8, align_bytes=64)
        h1_grouped = [
            regroup(h1, g, nc.vector.tensor_copy if g % 2 == 0 else nc.scalar.copy) for g in range(k2_passes)
        ]
        out_banks = [psum.tile([P, N_BANK], F32, name="out_%d" % n, tag="acc%d" % n) for n in range(n2_banks)]
        for g in range(k2_passes):
            quantise(h1_grouped[g], g, h1_codes, h1_planes)
            for n in range(n2_banks):
                cols = slice(N_BANK * n, N_BANK * (n + 1))
                nc.tensor.matmul_mx(
                    out=out_banks[n][:],
                    lhsT=h1_codes[:, g, :].bitcast(FP8X4),
                    lhsT_scale=h1_planes[:, g, :],
                    rhs=w2_codes[:, g, cols].bitcast(FP8X4),
                    rhs_scale=w2_planes[:, g, cols],
                    start=(g == 0),
                    stop=(g == k2_passes - 1),
                )
        for n in range(n2_banks):
            cols = slice(N_BANK * n, N_BANK * (n + 1))
            result = tail.tile([P, N_BANK], F32, tag="result", bufs=2)
            nc.vector.tensor_tensor(out=result[:], in0=out_banks[n][:], in1=b2_all[:, cols], op=ALU.add)
            nc.sync.dma_start(out=out[:, cols], in_=result[:])
